import numpy as np
import ml_dtypes


def mxq(x, axis, fmt="e4m3"):
    dtype, down = {"e4m3": (ml_dtypes.float8_e4m3fn, 7), "e5m2": (ml_dtypes.float8_e5m2, 14)}[fmt]
    v = np.moveaxis(np.asarray(x, np.float32).astype(ml_dtypes.bfloat16).astype(np.float64), axis, -1)
    blocks = v.reshape(v.shape[:-1] + (-1, 32))
    amax = np.abs(blocks).max(-1, keepdims=True)
    byte = np.maximum(np.where(amax > 0, np.frexp(amax)[1] - 1 + 127, 0) - down, 1)
    scale = np.exp2(byte - 127.0)
    codes = (blocks / scale).astype(np.float32).astype(dtype).astype(np.float64)
    return np.moveaxis((codes * scale).reshape(v.shape), -1, axis)


WIDE = False


def mx_kscale(k):
    if not WIDE:
        return np.ones(k)
    levels = np.array([10, -10, 5, -5, 0])
    if k % 512:
        return np.exp2(np.random.permutation(np.resize(levels, k // 32))).repeat(32)
    a = np.empty((k // 512, 16))
    for p in range(k // 512):
        a[p, :8] = np.random.permutation(np.resize(levels, 8))
        for g in range(8):
            far = levels[np.abs(levels - a[p, g]) >= 10]
            a[p, g + 8] = far[np.random.randint(len(far))]
    return np.exp2(a.ravel()).repeat(32)


BF16 = ml_dtypes.bfloat16


def bf(x):
    return np.asarray(x, np.float32).astype(BF16)


def f64(x):
    return np.asarray(x).astype(np.float64)


B, IN_C, OUT_C, HM, HN, NL = 256, 512, 512, 512, 16, 3


def leaky(v, leak):
    return np.where(v < 0, v * leak, v)


def setup_inputs():
    s = mx_kscale(IN_C)
    return {"x": bf(np.random.standard_normal((B, IN_C)) * s),
            "W_im": bf(np.random.standard_normal((HN, IN_C, HM)) * 0.7 / np.sqrt(IN_C) / s[None, :, None]),
            "W_in": bf(np.random.standard_normal((HM, IN_C, HN)) * 0.7 / np.sqrt(IN_C) / s[None, :, None]),
            "leak_m": bf(np.random.uniform(-2.0, 2.0, HM)),
            "leak_n": bf(np.random.uniform(-2.0, 2.0, HN))}


def core(x, W_im, W_in, leak_m, leak_n):
    xq = mxq(f64(x), 1, "e4m3")
    wim = mxq(f64(W_im), 1, "e4m3").transpose(1, 0, 2).reshape(IN_C, HN * HM)
    win = mxq(f64(W_in), 1, "e4m3").transpose(1, 0, 2).reshape(IN_C, HM * HN)
    x_m = leaky((xq @ wim).reshape(B, HN, HM), f64(leak_m))
    x_n = leaky((xq @ win).reshape(B, HM, HN), f64(leak_n))
    return x_m + x_n.transpose(0, 2, 1)


def e4m3fn_bytes(y):
    return np.clip(np.asarray(y, np.float64), -448.0, 448.0).astype(np.float32).astype(ml_dtypes.float8_e4m3fn).view(np.uint8)


def reference(x, W_im, W_in, leak_m, leak_n):
    out = core(x, W_im, W_in, leak_m, leak_n)
    s = np.max(np.abs(out)) / 448.0
    return out, e4m3fn_bytes(out / s)

@@ -1,0 +1,362 @@
+from contextlib import ExitStack
+
+import concourse.mybir as mybir
+from concourse.masks import make_identity
+
+F32 = mybir.dt.float32
+BF16 = mybir.dt.bfloat16
+U32 = mybir.dt.uint32
+U8 = mybir.dt.uint8
+FP8X4 = mybir.dt.float8_e4m3fn_x4
+FP8 = mybir.dt.float8_e4m3fn
+ALU = mybir.AluOpType
+ACT = mybir.ActivationFunctionType
+AX = mybir.AxisListType
+
+B, K, HM, HN = 256, 512, 512, 16
+P = 128
+BT = B // P
+MT = HM // P
+NU = HN // 2
+FLOPS = 2 * B * K * (2 * HN * HM)
+
+S_M = 384
+T2_ENGINES = "SSSV"
+REDUCE_DELAY = 3
+AHEAD = 2
+
+
+def tile_tensormoe_pa_kernel(tc, x, W_im, W_in, leak_m, leak_n, out_0, out_1):
+    nc = tc.nc
+    with ExitStack() as ctx:
+        const = ctx.enter_context(tc.tile_pool(name="const", bufs=1))
+        outp = ctx.enter_context(tc.tile_pool(name="outp", bufs=1))
+        psum = ctx.enter_context(tc.psum_pool(name="psum", bufs=4))
+
+        zeros = const.tile([P, 1], F32, name="zeros")
+        nc.vector.memset(zeros[:], 0.0)
+        warm = const.tile([P, 1], F32, name="warm")
+        nc.scalar.activation(out=warm[:], in_=zeros[:], func=ACT.Relu)
+        ident = const.tile([P, P], F32, name="ident")
+        make_identity(nc, ident[:])
+
+        cin = const.tile([P, MT, HN * P], U32, name="cin", align_bytes=64)
+        sc_in = const.tile([P, MT, HN * P], U8, name="sc_in", align_bytes=64)
+        cim = const.tile([P, HN * HM], U32, name="cim", align_bytes=64)
+        sc_im = const.tile([P, HN * HM], U8, name="sc_im", align_bytes=64)
+        xq = const.tile([P, B], U32, name="xq", align_bytes=64)
+        xs = const.tile([P, B], U8, name="xs", align_bytes=64)
+        dm = const.tile([P, HM], F32, name="dm")
+        en = const.tile([P, HN], F32, name="en")
+        stats = const.tile([P, HN + 2], F32, name="stats")
+        part = const.tile([P, 1], F32, name="part")
+        amax = const.tile([P, 1], F32, name="amax")
+        rec = const.tile([P, 1], F32, name="rec")
+        fac = const.tile([P, 1], F32, name="fac")
+
+        otile = {}
+        for nu in range(NU):
+            for bt in range(BT):
+                otile[(nu, bt)] = outp.tile([P, 2 * HM], F32, name="o%d_%d" % (nu, bt))
+
+        def oslice(n, bt):
+            return otile[(n // 2, bt)][:, (n % 2) * HM : (n % 2 + 1) * HM]
+
+        def xop(bt):
+            bs = slice(bt * P, (bt + 1) * P)
+            return xq[:, bs].bitcast(FP8X4), xs[:, bs]
+
+        sched = ctx.enter_context(tc.manual_schedule())
+
+        with ExitStack() as pctx:
+            prep = pctx.enter_context(tc.tile_pool(name="prep", bufs=1))
+            rawim_pool = pctx.enter_context(tc.tile_pool(name="rawim", bufs=3))
+            stgim_pool = pctx.enter_context(tc.tile_pool(name="stgim", bufs=1))
+            rawin_pool = pctx.enter_context(tc.tile_pool(name="rawin", bufs=2))
+            stgin_pool = pctx.enter_context(tc.tile_pool(name="stgin", bufs=2))
+
+            x_sb = prep.tile([P, BT, K], BF16, name="x_sb")
+            nc.sync.dma_start(out=x_sb[:], in_=x.rearrange("(t p) k -> p t k", p=P))
+            lrow = prep.tile([P, HM + HN], BF16, name="lrow")
+            nc.vector.memset(lrow[:], 0.0)
+            ones = prep.tile([P, P], BF16, name="ones")
+            nc.vector.memset(ones[:], 1.0)
+            nc.scalar.dma_start(out=lrow[0:1, 0:HM], in_=leak_m.rearrange("(o m) -> o m", o=1))
+            nc.scalar.dma_start(out=lrow[0:1, HM : HM + HN], in_=leak_n.rearrange("(o n) -> o n", o=1))
+
+            rawim = {}
+            rawin = {}
+            done_t3 = set()
+            done_blk = set()
+            order = [
+                ("im", 0), ("in", 0), ("im", 1), ("im", 2), ("in", 1), ("im", 3), ("in", 2),
+                ("im", 4), ("im", 5), ("in", 3), ("im", 6), ("im", 7),
+            ]
+            head = [0]
+
+            def pump():
+                while head[0] < len(order):
+                    kind, j = order[head[0]]
+                    if kind == "im":
+                        if j >= 3 and (j - 3) not in done_t3:
+                            return
+                        t = rawim_pool.tile([P, 2, 4, HM], BF16, name="rawim%d" % j, tag="rawim")
+                        nc.sync.dma_start(
+                            out=t[:], in_=W_im[2 * j : 2 * j + 2].rearrange("n (p j) m -> p n j m", j=4)
+                        )
+                        rawim[j] = t
+                    else:
+                        if j >= 2 and (2 * (j - 2) + 1) not in done_blk:
+                            return
+                        t = rawin_pool.tile([P, K * HN], BF16, name="rawin%d" % j, tag="rawin")
+                        half = K * HN // 2
+                        srcv = W_in[j * P : (j + 1) * P].rearrange("m i n -> m (i n)")
+                        for h in range(2):
+                            nc.sync.dma_start(
+                                out=t[:, h * half : (h + 1) * half], in_=srcv[:, h * half : (h + 1) * half]
+                            )
+                        rawin[j] = t
+                    head[0] += 1
+
+            pump()
+
+            xt = psum.tile([P, BT, 2, P], F32, name="xt", tag="tp")
+            for bt in range(BT):
+                xw = x_sb[:, bt, :].bitcast(F32)
+                for u in range(2):
+                    nc.tensor.transpose(xt[:, bt, u, :], xw[:, u::2], ident[:])
+            lmp = psum.tile([P, HM], F32, name="lmp", tag="pb")
+            nc.tensor.matmul(out=lmp[:], lhsT=ones[:], rhs=lrow[:, 0:HM], start=True, stop=True)
+            lnp = psum.tile([P, HN], F32, name="lnp", tag="pb")
+            nc.tensor.matmul(out=lnp[:], lhsT=ones[:], rhs=lrow[:, HM : HM + HN], start=True, stop=True)
+            gx = prep.tile([P, B * 4], BF16, name="gx", align_bytes=64)
+            nc.vector.tensor_copy(
+                out=gx[:].bitcast(F32).rearrange("p (t b u) -> p t b u", t=BT, u=2),
+                in_=xt[:].rearrange("p t u b -> p t b u"),
+            )
+            nc.vector.tensor_scalar(out=dm[:], in0=lmp[:], scalar1=-1.0, scalar2=None, op0=ALU.add)
+            nc.vector.quantize_mx(out=xq[:].bitcast(FP8X4), scales=xs[:], in_=gx[:])
+            nc.vector.tensor_scalar(out=en[:], in0=lnp[:], scalar1=-1.0, scalar2=1.0, op0=ALU.mult, op1=ALU.add)
+
+            stgim = {}
+
+            def interleave(eng, pair, g, nl, m0, m1):
+                src = rawim[pair][:, nl, :, m0:m1].rearrange("p j m -> p m j")
+                dst = g[:, nl * 4 * HM + 4 * m0 : nl * 4 * HM + 4 * m1].rearrange("p (m j) -> p m j", j=4)
+                if eng == "G":
+                    nc.gpsimd.tensor_scalar(out=dst, in0=src, scalar1=1.0, scalar2=0.0, op0=ALU.mult, op1=ALU.add)
+                elif eng == "S":
+                    nc.scalar.copy(out=dst, in_=src)
+                else:
+                    nc.vector.tensor_copy(out=dst, in_=src)
+
+            def new_stgim(pair):
+                stgim[pair] = stgim_pool.tile([P, 8 * HM], BF16, name="stgim%d" % pair, tag="stgim", align_bytes=64)
+                return stgim[pair]
+
+            def q_im(pair):
+                cs = slice(pair * 2 * HM, (pair + 1) * 2 * HM)
+                nc.vector.quantize_mx(out=cim[:, cs].bitcast(FP8X4), scales=sc_im[:, cs], in_=stgim[pair][:])
+
+            pbank = {}
+
+            def p_mm(pair):
+                for n in (2 * pair, 2 * pair + 1):
+                    cs = slice(n * HM, (n + 1) * HM)
+                    for bt in range(BT):
+                        lhsT, lsc = xop(bt)
+                        pb = psum.tile([P, HM], F32, name="pb%d_%d" % (n, bt), tag="pb")
+                        nc.tensor.matmul_mx(
+                            out=pb[:], lhsT=lhsT, lhsT_scale=lsc,
+                            rhs=cim[:, cs].bitcast(FP8X4), rhs_scale=sc_im[:, cs],
+                            start=True, stop=True,
+                        )
+                        pbank[(n, bt)] = pb
+
+            def b_pass(n):
+                for bt in range(BT):
+                    nc.vector.scalar_tensor_tensor(
+                        out=oslice(n, bt), in0=pbank[(n, bt)][:], scalar=0.0, in1=dm[:],
+                        op0=ALU.min, op1=ALU.mult,
+                    )
+
+            tbank = {}
+            stgin = {}
+
+            def t2_transposes(blk):
+                mt, h = blk // 2, blk % 2
+                words = rawin[mt][:].bitcast(F32)
+                for r in range(4):
+                    nu = 4 * h + r
+                    tp = psum.tile([P, 4, P], F32, name="tp%d_%d" % (mt, nu), tag="tp")
+                    for t in range(4):
+                        nc.tensor.transpose(tp[:, t, :], words[:, 8 * t + nu :: 32], ident[:])
+                    tbank[(blk, r)] = tp
+                done_blk.add(blk)
+                pump()
+
+            def t2_copy(blk, r):
+                if r == 0:
+                    stgin[blk] = stgin_pool.tile([P, 4096], BF16, name="stgin%d" % blk, tag="stgin", align_bytes=64)
+                tp = tbank[(blk, r)]
+                src = tp[:].rearrange("p t m -> p (t m)").bitcast(BF16).rearrange("p (t m e) -> p e m t", t=4, e=2)
+                dst = stgin[blk][:, r * 1024 : (r + 1) * 1024].rearrange("p (e m t) -> p e m t", e=2, t=4)
+                if T2_ENGINES[r] == "S":
+                    nc.scalar.copy(out=dst, in_=src)
+                else:
+                    nc.vector.tensor_copy(out=dst, in_=src)
+
+            def q_in(blk):
+                mt, h = blk // 2, blk % 2
+                cs = slice(h * 1024, (h + 1) * 1024)
+                nc.vector.quantize_mx(out=cin[:, mt, cs].bitcast(FP8X4), scales=sc_in[:, mt, cs], in_=stgin[blk][:])
+
+            g = new_stgim(0)
+            interleave("V", 0, g, 0, 0, HM)
+            interleave("S", 0, g, 1, 0, HM // 2)
+            interleave("G", 0, g, 1, HM // 2, HM)
+            done_t3.add(0)
+            pump()
+            for k in range(NU):
+                t2_transposes(k)
+                if k >= 1:
+                    q_in(k - 1)
+                q_im(k)
+                p_mm(k)
+                for r in range(4):
+                    if T2_ENGINES[r] == "S":
+                        t2_copy(k, r)
+                if k + 1 < NU:
+                    g = new_stgim(k + 1)
+                    interleave("G", k + 1, g, 1, 0, HM)
+                    interleave("G", k + 1, g, 0, S_M, HM)
+                    interleave("S", k + 1, g, 0, 0, S_M)
+                    done_t3.add(k + 1)
+                    pump()
+                for r in range(4):
+                    if T2_ENGINES[r] != "S":
+                        t2_copy(k, r)
+                b_pass(2 * k)
+                if k + 1 < NU:
+                    b_pass(2 * k + 1)
+            q_in(NU - 1)
+            b_pass(2 * NU - 1)
+
+        with tc.tile_pool(name="tmp", bufs=3) as tmp:
+            banks = {}
+
+            def mm(j):
+                n, bt = j // 2, j % 2
+                lhsT, lsc = xop(bt)
+                qb = psum.tile([P, HM], F32, name="qb%d_%d" % (n, bt), tag="tp")
+                sb = psum.tile([P, HM], F32, name="sb%d_%d" % (n, bt), tag="pb")
+                ns = slice(n * P, (n + 1) * P)
+                for mt in range(MT):
+                    ms = slice(mt * P, (mt + 1) * P)
+                    nc.tensor.matmul_mx(
+                        out=qb[:, ms], lhsT=lhsT, lhsT_scale=lsc,
+                        rhs=cin[:, mt, ns].bitcast(FP8X4), rhs_scale=sc_in[:, mt, ns],
+                        start=True, stop=True,
+                    )
+                for mt in range(MT):
+                    ms = slice(mt * P, (mt + 1) * P)
+                    cs = slice(n * HM + mt * P, n * HM + (mt + 1) * P)
+                    nc.tensor.matmul_mx(
+                        out=sb[:, ms], lhsT=lhsT, lhsT_scale=lsc,
+                        rhs=cim[:, cs].bitcast(FP8X4), rhs_scale=sc_im[:, cs],
+                        start=True, stop=False,
+                    )
+                    nc.tensor.matmul_mx(
+                        out=sb[:, ms], lhsT=lhsT, lhsT_scale=lsc,
+                        rhs=cin[:, mt, ns].bitcast(FP8X4), rhs_scale=sc_in[:, mt, ns],
+                        start=False, stop=True,
+                    )
+                nq = tmp.tile([P, HM], F32, name="nq%d_%d" % (n, bt), tag="nq")
+                nc.scalar.activation(out=nq[:], in_=qb[:], func=ACT.Relu, scale=-1.0)
+                banks[j] = (nq, sb)
+
+            def epi(j):
+                n, bt = j // 2, j % 2
+                nq, sb = banks[j]
+                uu = tmp.tile([P, HM], F32, name="uu%d_%d" % (n, bt), tag="uu")
+                nc.vector.scalar_tensor_tensor(
+                    out=uu[:], in0=nq[:], scalar=en[:, n : n + 1], in1=sb[:], op0=ALU.mult, op1=ALU.add
+                )
+                osl = oslice(n, bt)
+                nc.gpsimd.tensor_tensor(out=osl, in0=uu[:], in1=osl, op=ALU.add)
+
+            def finish(j):
+                nu, bt = j // 4, j % 2
+                o = otile[(nu, bt)]
+                if nu < NU - 1:
+                    c = nu * BT + bt
+                    src = o[:]
+                else:
+                    c = (NU - 1) * BT + j % 4
+                    src = oslice(j // 2, bt)
+                nc.vector.tensor_reduce(
+                    out=stats[:, c : c + 1], in_=src, axis=AX.X, op=ALU.max, apply_absolute_value=True
+                )
+                if j % 4 >= 2:
+                    nc.sync.dma_start(
+                        out=out_0[bt * P : (bt + 1) * P, 2 * nu : 2 * nu + 2, :].rearrange("b n m -> b (n m)"),
+                        in_=o[:],
+                    )
+
+            NJ = HN * BT
+            for j in range(AHEAD):
+                mm(j)
+            pending = []
+            served = 0
+            for j in range(NJ):
+                if j + AHEAD < NJ:
+                    mm(j + AHEAD)
+                epi(j)
+                if j % 4 >= 2 or j // 4 == NU - 1:
+                    pending.append((j + REDUCE_DELAY, j))
+                while served < len(pending) and pending[served][0] <= j:
+                    finish(pending[served][1])
+                    served += 1
+            for item in pending[served:]:
+                finish(item[1])
+
+        nc.vector.tensor_reduce(out=part[:], in_=stats[:], axis=AX.X, op=ALU.max)
+        pt = psum.tile([P, P], F32, name="pt", tag="tp")
+        nc.tensor.transpose(pt[:], part[:, 0:1].to_broadcast([P, P]), ident[:])
+        nc.vector.tensor_reduce(out=amax[:], in_=pt[:], axis=AX.X, op=ALU.max)
+        nc.vector.reciprocal(out=rec[:], in_=amax[:])
+        nc.vector.tensor_scalar(out=fac[:], in0=rec[:], scalar1=448.0, scalar2=None, op0=ALU.mult)
+
+        with tc.tile_pool(name="f8p", bufs=1) as f8p:
+            k = 0
+            for bt in range(BT):
+                for h in range(2):
+                    f8 = f8p.tile([P, 4096], FP8, name="f8_%d_%d" % (bt, h))
+                    for q in range(4):
+                        o = otile[(4 * h + q, bt)]
+                        dst = f8[:, q * 1024 : (q + 1) * 1024]
+                        if k % 3 == 2:
+                            nc.scalar.activation(
+                                out=dst, in_=o[:], func=ACT.Identity, scale=fac[:, 0:1], bias=zeros[:, 0:1],
+                                saturate=False,
+                            )
+                        else:
+                            nc.vector.tensor_scalar(
+                                out=dst, in0=o[:], scalar1=fac[:, 0:1], scalar2=None, op0=ALU.mult, saturate=False
+                            )
+                        k += 1
+                        if k == 14:
+                            nc.sync.dma_start(
+                                out=out_1[bt * P : (bt + 1) * P, 8 * h : 8 * h + 4, :].rearrange("b n m -> b (n m)"),
+                                in_=f8[:, 0:2048].bitcast(U8),
+                            )
+                    if k < 16:
+                        nc.sync.dma_start(
+                            out=out_1[bt * P : (bt + 1) * P, 8 * h : 8 * h + 8, :].rearrange("b n m -> b (n m)"),
+                            in_=f8[:].bitcast(U8),
+                        )
+                    else:
+                        nc.sync.dma_start(
+                            out=out_1[bt * P : (bt + 1) * P, 8 * h + 4 : 8 * h + 8, :].rearrange("b n m -> b (n m)"),
+                            in_=f8[:, 2048:4096].bitcast(U8),
+                        )

@@ -81,8 +81,8 @@ def tile_tensormoe_pa_kernel(tc, x, W_im, W_in, leak_m, leak_n, out_0, out_1):
             nc.vector.memset(lrow[:], 0.0)
             ones = prep.tile([P, P], BF16, name="ones")
             nc.vector.memset(ones[:], 1.0)
-            nc.scalar.dma_start(out=lrow[0:1, 0:HM], in_=leak_m.rearrange("(o m) -> o m", o=1))
-            nc.scalar.dma_start(out=lrow[0:1, HM : HM + HN], in_=leak_n.rearrange("(o n) -> o n", o=1))
+            nc.sync.dma_start(out=lrow[0:1, 0:HM], in_=leak_m.rearrange("(o m) -> o m", o=1))
+            nc.sync.dma_start(out=lrow[0:1, HM : HM + HN], in_=leak_n.rearrange("(o n) -> o n", o=1))
 
             rawim = {}
             rawin = {}
@@ -141,8 +141,8 @@ def tile_tensormoe_pa_kernel(tc, x, W_im, W_in, leak_m, leak_n, out_0, out_1):
             stgim = {}
 
             def interleave(eng, pair, g, nl, m0, m1):
-                src = rawim[pair][:, nl, :, m0:m1].rearrange("p j m -> p m j")
-                dst = g[:, nl * 4 * HM + 4 * m0 : nl * 4 * HM + 4 * m1].rearrange("p (m j) -> p m j", j=4)
+                src = rawim[pair][:, nl, :, m0:m1].rearrange("p j (c i) -> p c j i", i=4)
+                dst = g[:, nl * 4 * HM + 4 * m0 : nl * 4 * HM + 4 * m1].rearrange("p (c i j) -> p c j i", i=4, j=4)
                 if eng == "G":
                     nc.gpsimd.tensor_scalar(out=dst, in0=src, scalar1=1.0, scalar2=0.0, op0=ALU.mult, op1=ALU.add)
                 elif eng == "S":

@@ -144,6 +144,8 @@ def tile_tensormoe_pa_kernel(tc, x, W_im, W_in, leak_m, leak_n, out_0, out_1):
                 src = rawim[pair][:, nl, :, m0:m1].rearrange("p j (c i) -> p c j i", i=4)
                 dst = g[:, nl * 4 * HM + 4 * m0 : nl * 4 * HM + 4 * m1].rearrange("p (c i j) -> p c j i", i=4, j=4)
                 if eng == "G":
+                    src = rawim[pair][:, nl, :, m0:m1].rearrange("p j m -> p m j")
+                    dst = g[:, nl * 4 * HM + 4 * m0 : nl * 4 * HM + 4 * m1].rearrange("p (m j) -> p m j", j=4)
                     nc.gpsimd.tensor_scalar(out=dst, in0=src, scalar1=1.0, scalar2=0.0, op0=ALU.mult, op1=ALU.add)
                 elif eng == "S":
                     nc.scalar.copy(out=dst, in_=src)

@@ -24,6 +24,7 @@ S_M = 384
 T2_ENGINES = "SSSV"
 REDUCE_DELAY = 3
 AHEAD = 2
+WIDE = True
 
 
 def tile_tensormoe_pa_kernel(tc, x, W_im, W_in, leak_m, leak_n, out_0, out_1):
@@ -144,8 +145,6 @@ def tile_tensormoe_pa_kernel(tc, x, W_im, W_in, leak_m, leak_n, out_0, out_1):
                 src = rawim[pair][:, nl, :, m0:m1].rearrange("p j (c i) -> p c j i", i=4)
                 dst = g[:, nl * 4 * HM + 4 * m0 : nl * 4 * HM + 4 * m1].rearrange("p (c i j) -> p c j i", i=4, j=4)
                 if eng == "G":
-                    src = rawim[pair][:, nl, :, m0:m1].rearrange("p j m -> p m j")
-                    dst = g[:, nl * 4 * HM + 4 * m0 : nl * 4 * HM + 4 * m1].rearrange("p (m j) -> p m j", j=4)
                     nc.gpsimd.tensor_scalar(out=dst, in0=src, scalar1=1.0, scalar2=0.0, op0=ALU.mult, op1=ALU.add)
                 elif eng == "S":
                     nc.scalar.copy(out=dst, in_=src)
@@ -197,13 +196,13 @@ def tile_tensormoe_pa_kernel(tc, x, W_im, W_in, leak_m, leak_n, out_0, out_1):
                 done_blk.add(blk)
                 pump()
 
-            def t2_copy(blk, r):
+            def t2_copy(blk, r, eng=None):
                 if r == 0:
                     stgin[blk] = stgin_pool.tile([P, 4096], BF16, name="stgin%d" % blk, tag="stgin", align_bytes=64)
                 tp = tbank[(blk, r)]
                 src = tp[:].rearrange("p t m -> p (t m)").bitcast(BF16).rearrange("p (t m e) -> p e m t", t=4, e=2)
                 dst = stgin[blk][:, r * 1024 : (r + 1) * 1024].rearrange("p (e m t) -> p e m t", e=2, t=4)
-                if T2_ENGINES[r] == "S":
+                if (eng or T2_ENGINES[r]) == "S":
                     nc.scalar.copy(out=dst, in_=src)
                 else:
                     nc.vector.tensor_copy(out=dst, in_=src)
@@ -213,42 +212,14 @@ def tile_tensormoe_pa_kernel(tc, x, W_im, W_in, leak_m, leak_n, out_0, out_1):
                 cs = slice(h * 1024, (h + 1) * 1024)
                 nc.vector.quantize_mx(out=cin[:, mt, cs].bitcast(FP8X4), scales=sc_in[:, mt, cs], in_=stgin[blk][:])
 
-            g = new_stgim(0)
-            interleave("V", 0, g, 0, 0, HM)
-            interleave("S", 0, g, 1, 0, HM // 2)
-            interleave("G", 0, g, 1, HM // 2, HM)
-            done_t3.add(0)
-            pump()
-            for k in range(NU):
-                t2_transposes(k)
-                if k >= 1:
-                    q_in(k - 1)
-                q_im(k)
-                p_mm(k)
-                for r in range(4):
-                    if T2_ENGINES[r] == "S":
-                        t2_copy(k, r)
-                if k + 1 < NU:
-                    g = new_stgim(k + 1)
-                    interleave("G", k + 1, g, 1, 0, HM)
-                    interleave("G", k + 1, g, 0, S_M, HM)
-                    interleave("S", k + 1, g, 0, 0, S_M)
-                    done_t3.add(k + 1)
-                    pump()
-                for r in range(4):
-                    if T2_ENGINES[r] != "S":
-                        t2_copy(k, r)
-                b_pass(2 * k)
-                if k + 1 < NU:
-                    b_pass(2 * k + 1)
-            q_in(NU - 1)
-            b_pass(2 * NU - 1)
-
-        with tc.tile_pool(name="tmp", bufs=3) as tmp:
             banks = {}
+            rings = {}
+
+            def tile_of(j):
+                return 2 * (j // 4) + j % 2, (j % 4) // 2
 
             def mm(j):
-                n, bt = j // 2, j % 2
+                n, bt = tile_of(j)
                 lhsT, lsc = xop(bt)
                 qb = psum.tile([P, HM], F32, name="qb%d_%d" % (n, bt), tag="tp")
                 sb = psum.tile([P, HM], F32, name="sb%d_%d" % (n, bt), tag="pb")
@@ -273,38 +244,99 @@ def tile_tensormoe_pa_kernel(tc, x, W_im, W_in, leak_m, leak_n, out_0, out_1):
                         rhs=cin[:, mt, ns].bitcast(FP8X4), rhs_scale=sc_in[:, mt, ns],
                         start=False, stop=True,
                     )
-                nq = tmp.tile([P, HM], F32, name="nq%d_%d" % (n, bt), tag="nq")
-                nc.scalar.activation(out=nq[:], in_=qb[:], func=ACT.Relu, scale=-1.0)
+                nq = rings["nq"][:, j % 4, :]
+                nc.scalar.activation(out=nq, in_=qb[:], func=ACT.Relu, scale=-1.0)
                 banks[j] = (nq, sb)
 
             def epi(j):
-                n, bt = j // 2, j % 2
+                n, bt = tile_of(j)
                 nq, sb = banks[j]
-                uu = tmp.tile([P, HM], F32, name="uu%d_%d" % (n, bt), tag="uu")
+                uu = rings["uu"][:, (j // 2) % 2, :]
+                hs = slice((n % 2) * HM, (n % 2 + 1) * HM)
                 nc.vector.scalar_tensor_tensor(
-                    out=uu[:], in0=nq[:], scalar=en[:, n : n + 1], in1=sb[:], op0=ALU.mult, op1=ALU.add
+                    out=uu[:, hs], in0=nq, scalar=en[:, n : n + 1], in1=sb[:], op0=ALU.mult, op1=ALU.add
                 )
-                osl = oslice(n, bt)
-                nc.gpsimd.tensor_tensor(out=osl, in0=uu[:], in1=osl, op=ALU.add)
+                if j // 4 == NU - 1 or not WIDE:
+                    osl = oslice(n, bt)
+                    nc.gpsimd.tensor_tensor(out=osl, in0=uu[:, hs], in1=osl, op=ALU.add)
+                elif j % 2 == 1:
+                    o = otile[(n // 2, bt)]
+                    nc.gpsimd.tensor_tensor(out=o[:], in0=uu, in1=o[:], op=ALU.add)
 
             def finish(j):
-                nu, bt = j // 4, j % 2
+                n, bt = tile_of(j)
+                nu = n // 2
                 o = otile[(nu, bt)]
                 if nu < NU - 1:
                     c = nu * BT + bt
                     src = o[:]
                 else:
                     c = (NU - 1) * BT + j % 4
-                    src = oslice(j // 2, bt)
+                    src = oslice(n, bt)
                 nc.vector.tensor_reduce(
                     out=stats[:, c : c + 1], in_=src, axis=AX.X, op=ALU.max, apply_absolute_value=True
                 )
-                if j % 4 >= 2:
+                if j % 2 == 1:
                     nc.sync.dma_start(
                         out=out_0[bt * P : (bt + 1) * P, 2 * nu : 2 * nu + 2, :].rearrange("b n m -> b (n m)"),
                         in_=o[:],
                     )
 
+            def p_one(n, bt):
+                cs = slice(n * HM, (n + 1) * HM)
+                lhsT, lsc = xop(bt)
+                pb = psum.tile([P, HM], F32, name="pb%d_%d" % (n, bt), tag="pb")
+                nc.tensor.matmul_mx(
+                    out=pb[:], lhsT=lhsT, lhsT_scale=lsc,
+                    rhs=cim[:, cs].bitcast(FP8X4), rhs_scale=sc_im[:, cs],
+                    start=True, stop=True,
+                )
+                pbank[(n, bt)] = pb
+
+            def b_one(n, bt):
+                nc.vector.scalar_tensor_tensor(
+                    out=oslice(n, bt), in0=pbank[(n, bt)][:], scalar=0.0, in1=dm[:],
+                    op0=ALU.min, op1=ALU.mult,
+                )
+
+            g = new_stgim(0)
+            interleave("V", 0, g, 0, 0, HM)
+            interleave("S", 0, g, 1, 0, HM // 2)
+            interleave("G", 0, g, 1, HM // 2, HM)
+            done_t3.add(0)
+            pump()
+            for k in range(NU - 1):
+                t2_transposes(k)
+                if k >= 1:
+                    q_in(k - 1)
+                q_im(k)
+                p_mm(k)
+                for r in range(4):
+                    if T2_ENGINES[r] == "S":
+                        t2_copy(k, r)
+                g = new_stgim(k + 1)
+                interleave("G", k + 1, g, 1, 0, HM)
+                interleave("G", k + 1, g, 0, S_M, HM)
+                interleave("S", k + 1, g, 0, 0, S_M)
+                done_t3.add(k + 1)
+                pump()
+                for r in range(4):
+                    if T2_ENGINES[r] != "S":
+                        t2_copy(k, r)
+                b_pass(2 * k)
+                b_pass(2 * k + 1)
+
+            k = NU - 1
+            t2_transposes(k)
+            q_in(k - 1)
+            q_im(k)
+            rings["nq"] = rawim_pool.tile([P, 4, HM], F32, name="nqring", tag="rawim")
+            rings["uu"] = rawim_pool.tile([P, 2, 2 * HM], F32, name="uuring", tag="rawim")
+            for r in range(4):
+                t2_copy(k, r, "S")
+            q_in(k)
+
+            late = [(2 * k, 0), (2 * k, 1), (2 * k + 1, 0), (2 * k + 1, 1)]
             NJ = HN * BT
             for j in range(AHEAD):
                 mm(j)
@@ -314,7 +346,11 @@ def tile_tensormoe_pa_kernel(tc, x, W_im, W_in, leak_m, leak_n, out_0, out_1):
                 if j + AHEAD < NJ:
                     mm(j + AHEAD)
                 epi(j)
-                if j % 4 >= 2 or j // 4 == NU - 1:
+                if j % 2 == 1 and j - 1 < len(late):
+                    for n, bt in late[j - 1 : j + 1]:
+                        p_one(n, bt)
+                        b_one(n, bt)
+                if j % 2 == 1 or j // 4 == NU - 1:
                     pending.append((j + REDUCE_DELAY, j))
                 while served < len(pending) and pending[served][0] <= j:
                     finish(pending[served][1])

@@ -24,6 +24,11 @@ S_M = 384
 T2_ENGINES = "SSSV"
 REDUCE_DELAY = 3
 AHEAD = 2
+NL1 = 7
+TB = [None, 0, 1, 2, 3, 4, 6]
+LATE = [5, 7]
+J_BANK = [1, 2, 4, 5, 7, 8, 10, 11]
+J_QIN = 13
 WIDE = True
 
 
@@ -76,7 +81,7 @@ def tile_tensormoe_pa_kernel(tc, x, W_im, W_in, leak_m, leak_n, out_0, out_1):
             rawin_pool = pctx.enter_context(tc.tile_pool(name="rawin", bufs=2))
             stgin_pool = pctx.enter_context(tc.tile_pool(name="stgin", bufs=2))
 
-            x_sb = prep.tile([P, BT, K], BF16, name="x_sb")
+            x_sb = prep.tile([P, BT, K], BF16, name="x_sb", tag="pa", align_bytes=64)
             nc.sync.dma_start(out=x_sb[:], in_=x.rearrange("(t p) k -> p t k", p=P))
             lrow = prep.tile([P, HM + HN], BF16, name="lrow")
             nc.vector.memset(lrow[:], 0.0)
@@ -90,8 +95,8 @@ def tile_tensormoe_pa_kernel(tc, x, W_im, W_in, leak_m, leak_n, out_0, out_1):
             done_t3 = set()
             done_blk = set()
             order = [
-                ("im", 0), ("in", 0), ("im", 1), ("im", 2), ("in", 1), ("im", 3), ("in", 2),
-                ("im", 4), ("im", 5), ("in", 3), ("im", 6), ("im", 7),
+                ("im", 0), ("im", 1), ("in", 0), ("im", 2), ("im", 3), ("in", 1), ("im", 4), ("in", 2),
+                ("im", 5), ("im", 6), ("in", 3), ("im", 7),
             ]
             head = [0]
 
@@ -130,7 +135,7 @@ def tile_tensormoe_pa_kernel(tc, x, W_im, W_in, leak_m, leak_n, out_0, out_1):
             nc.tensor.matmul(out=lmp[:], lhsT=ones[:], rhs=lrow[:, 0:HM], start=True, stop=True)
             lnp = psum.tile([P, HN], F32, name="lnp", tag="pb")
             nc.tensor.matmul(out=lnp[:], lhsT=ones[:], rhs=lrow[:, HM : HM + HN], start=True, stop=True)
-            gx = prep.tile([P, B * 4], BF16, name="gx", align_bytes=64)
+            gx = prep.tile([P, B * 4], BF16, name="gx", tag="pc", align_bytes=64)
             nc.vector.tensor_copy(
                 out=gx[:].bitcast(F32).rearrange("p (t b u) -> p t b u", t=BT, u=2),
                 in_=xt[:].rearrange("p t u b -> p t b u"),
@@ -196,6 +201,15 @@ def tile_tensormoe_pa_kernel(tc, x, W_im, W_in, leak_m, leak_n, out_0, out_1):
                 done_blk.add(blk)
                 pump()
 
+            def t2_tr_one(blk, r):
+                mt, h = blk // 2, blk % 2
+                words = rawin[mt][:].bitcast(F32)
+                nu = 4 * h + r
+                tp = psum.tile([P, 4, P], F32, name="tp%d_%d" % (mt, nu), tag="tp")
+                for t in range(4):
+                    nc.tensor.transpose(tp[:, t, :], words[:, 8 * t + nu :: 32], ident[:])
+                tbank[(blk, r)] = tp
+
             def t2_copy(blk, r, eng=None):
                 if r == 0:
                     stgin[blk] = stgin_pool.tile([P, 4096], BF16, name="stgin%d" % blk, tag="stgin", align_bytes=64)
@@ -244,7 +258,8 @@ def tile_tensormoe_pa_kernel(tc, x, W_im, W_in, leak_m, leak_n, out_0, out_1):
                         rhs=cin[:, mt, ns].bitcast(FP8X4), rhs_scale=sc_in[:, mt, ns],
                         start=False, stop=True,
                     )
-                nq = rings["nq"][:, j % 4, :]
+                nqt = prep.tile([P, HM], F32, name="nq%d" % j, tag="pa" if j % 2 == 0 else "pc", align_bytes=64)
+                nq = nqt[:]
                 nc.scalar.activation(out=nq, in_=qb[:], func=ACT.Relu, scale=-1.0)
                 banks[j] = (nq, sb)
 
@@ -305,39 +320,55 @@ def tile_tensormoe_pa_kernel(tc, x, W_im, W_in, leak_m, leak_n, out_0, out_1):
             interleave("G", 0, g, 1, HM // 2, HM)
             done_t3.add(0)
             pump()
-            for k in range(NU - 1):
-                t2_transposes(k)
-                if k >= 1:
-                    q_in(k - 1)
+            for k in range(NL1):
+                if TB[k] is not None:
+                    t2_transposes(TB[k])
+                if k >= 1 and TB[k - 1] is not None:
+                    q_in(TB[k - 1])
                 q_im(k)
                 p_mm(k)
-                for r in range(4):
-                    if T2_ENGINES[r] == "S":
-                        t2_copy(k, r)
+                if TB[k] is not None:
+                    for r in range(4):
+                        if T2_ENGINES[r] == "S":
+                            t2_copy(TB[k], r)
                 g = new_stgim(k + 1)
                 interleave("G", k + 1, g, 1, 0, HM)
                 interleave("G", k + 1, g, 0, S_M, HM)
                 interleave("S", k + 1, g, 0, 0, S_M)
                 done_t3.add(k + 1)
                 pump()
-                for r in range(4):
-                    if T2_ENGINES[r] != "S":
-                        t2_copy(k, r)
+                if TB[k] is not None:
+                    for r in range(4):
+                        if T2_ENGINES[r] != "S":
+                            t2_copy(TB[k], r)
                 b_pass(2 * k)
                 b_pass(2 * k + 1)
 
-            k = NU - 1
-            t2_transposes(k)
-            q_in(k - 1)
+            k = NL1
+            q_in(TB[k - 1])
             q_im(k)
-            rings["nq"] = rawim_pool.tile([P, 4, HM], F32, name="nqring", tag="rawim")
             rings["uu"] = rawim_pool.tile([P, 2, 2 * HM], F32, name="uuring", tag="rawim")
-            for r in range(4):
-                t2_copy(k, r, "S")
-            q_in(k)
 
-            late = [(2 * k, 0), (2 * k, 1), (2 * k + 1, 0), (2 * k + 1, 1)]
             NJ = HN * BT
+            fill = {}
+
+            def at(j, f):
+                fill.setdefault(j, []).append(f)
+
+            def first_pass(n, bt):
+                p_one(n, bt)
+                b_one(n, bt)
+
+            for q, (n, bt) in enumerate([(2 * k, 0), (2 * k + 1, 0), (2 * k, 1), (2 * k + 1, 1)]):
+                at(q, lambda n=n, bt=bt: p_one(n, bt))
+                at(q + 1, lambda n=n, bt=bt: b_one(n, bt))
+            for q in range(8):
+                blk, r = LATE[q // 4], q % 4
+                at(J_BANK[q] - 1, lambda blk=blk, r=r: t2_tr_one(blk, r))
+                at(J_BANK[q], lambda blk=blk, r=r: t2_copy(blk, r, "S"))
+            at(J_QIN, lambda: q_in(LATE[0]))
+            at(J_QIN, lambda: q_in(LATE[1]))
+
             for j in range(AHEAD):
                 mm(j)
             pending = []
@@ -346,15 +377,13 @@ def tile_tensormoe_pa_kernel(tc, x, W_im, W_in, leak_m, leak_n, out_0, out_1):
                 if j + AHEAD < NJ:
                     mm(j + AHEAD)
                 epi(j)
-                if j % 2 == 1 and j - 1 < len(late):
-                    for n, bt in late[j - 1 : j + 1]:
-                        p_one(n, bt)
-                        b_one(n, bt)
                 if j % 2 == 1 or j // 4 == NU - 1:
                     pending.append((j + REDUCE_DELAY, j))
                 while served < len(pending) and pending[served][0] <= j:
                     finish(pending[served][1])
                     served += 1
+                for f in fill.get(j, []):
+                    f()
             for item in pending[served:]:
                 finish(item[1])
 

@@ -20,7 +20,7 @@ MT = HM // P
 NU = HN // 2
 FLOPS = 2 * B * K * (2 * HN * HM)
 
-S_M = 384
+S_M = 448
 T2_ENGINES = "SSSV"
 REDUCE_DELAY = 3
 AHEAD = 2

@@ -29,7 +29,7 @@ TB = [None, 0, 1, 2, 3, 4, 6]
 LATE = [5, 7]
 J_BANK = [1, 2, 4, 5, 7, 8, 10, 11]
 J_QIN = 13
-WIDE = True
+WIDE = False
 
 
 def tile_tensormoe_pa_kernel(tc, x, W_im, W_in, leak_m, leak_n, out_0, out_1):

@@ -20,10 +20,11 @@ MT = HM // P
 NU = HN // 2
 FLOPS = 2 * B * K * (2 * HN * HM)
 
-S_M = 448
+S_M = 384
 T2_ENGINES = "SSSV"
 REDUCE_DELAY = 3
 AHEAD = 2
+V_STEPS = (1, 3, 5)
 NL1 = 7
 TB = [None, 0, 1, 2, 3, 4, 6]
 LATE = [5, 7]
@@ -329,8 +330,8 @@ def tile_tensormoe_pa_kernel(tc, x, W_im, W_in, leak_m, leak_n, out_0, out_1):
                 p_mm(k)
                 if TB[k] is not None:
                     for r in range(4):
-                        if T2_ENGINES[r] == "S":
-                            t2_copy(TB[k], r)
+                        if T2_ENGINES[r] == "S" or k not in V_STEPS:
+                            t2_copy(TB[k], r, "S")
                 g = new_stgim(k + 1)
                 interleave("G", k + 1, g, 1, 0, HM)
                 interleave("G", k + 1, g, 0, S_M, HM)
@@ -339,7 +340,7 @@ def tile_tensormoe_pa_kernel(tc, x, W_im, W_in, leak_m, leak_n, out_0, out_1):
                 pump()
                 if TB[k] is not None:
                     for r in range(4):
-                        if T2_ENGINES[r] != "S":
+                        if T2_ENGINES[r] != "S" and k in V_STEPS:
                             t2_copy(TB[k], r)
                 b_pass(2 * k)
                 b_pass(2 * k + 1)

@@ -61,10 +61,13 @@ def tile_tensormoe_pa_kernel(tc, x, W_im, W_in, leak_m, leak_n, out_0, out_1):
         rec = const.tile([P, 1], F32, name="rec")
         fac = const.tile([P, 1], F32, name="fac")
 
+        obig = []
+        for bt in range(BT):
+            obig.append(outp.tile([P, HN * HM], F32, name="obig%d" % bt))
         otile = {}
         for nu in range(NU):
             for bt in range(BT):
-                otile[(nu, bt)] = outp.tile([P, 2 * HM], F32, name="o%d_%d" % (nu, bt))
+                otile[(nu, bt)] = obig[bt][:, nu * 2 * HM : (nu + 1) * 2 * HM]
 
         def oslice(n, bt):
             return otile[(n // 2, bt)][:, (n % 2) * HM : (n % 2 + 1) * HM]
@@ -277,7 +280,7 @@ def tile_tensormoe_pa_kernel(tc, x, W_im, W_in, leak_m, leak_n, out_0, out_1):
                     nc.gpsimd.tensor_tensor(out=osl, in0=uu[:, hs], in1=osl, op=ALU.add)
                 elif j % 2 == 1:
                     o = otile[(n // 2, bt)]
-                    nc.gpsimd.tensor_tensor(out=o[:], in0=uu, in1=o[:], op=ALU.add)
+                    nc.gpsimd.tensor_tensor(out=o, in0=uu, in1=o, op=ALU.add)
 
             def finish(j):
                 n, bt = tile_of(j)
@@ -285,7 +288,7 @@ def tile_tensormoe_pa_kernel(tc, x, W_im, W_in, leak_m, leak_n, out_0, out_1):
                 o = otile[(nu, bt)]
                 if nu < NU - 1:
                     c = nu * BT + bt
-                    src = o[:]
+                    src = o
                 else:
                     c = (NU - 1) * BT + j % 4
                     src = oslice(n, bt)
@@ -295,7 +298,7 @@ def tile_tensormoe_pa_kernel(tc, x, W_im, W_in, leak_m, leak_n, out_0, out_1):
                 if j % 2 == 1:
                     nc.sync.dma_start(
                         out=out_0[bt * P : (bt + 1) * P, 2 * nu : 2 * nu + 2, :].rearrange("b n m -> b (n m)"),
-                        in_=o[:],
+                        in_=o,
                     )
 
             def p_one(n, bt):
@@ -396,35 +399,45 @@ def tile_tensormoe_pa_kernel(tc, x, W_im, W_in, leak_m, leak_n, out_0, out_1):
         nc.vector.tensor_scalar(out=fac[:], in0=rec[:], scalar1=448.0, scalar2=None, op0=ALU.mult)
 
         with tc.tile_pool(name="f8p", bufs=1) as f8p:
-            k = 0
+            half = HN * HM // 2
+            f8 = {}
             for bt in range(BT):
                 for h in range(2):
-                    f8 = f8p.tile([P, 4096], FP8, name="f8_%d_%d" % (bt, h))
-                    for q in range(4):
-                        o = otile[(4 * h + q, bt)]
-                        dst = f8[:, q * 1024 : (q + 1) * 1024]
-                        if k % 3 == 2:
-                            nc.scalar.activation(
-                                out=dst, in_=o[:], func=ACT.Identity, scale=fac[:, 0:1], bias=zeros[:, 0:1],
-                                saturate=False,
-                            )
-                        else:
-                            nc.vector.tensor_scalar(
-                                out=dst, in0=o[:], scalar1=fac[:, 0:1], scalar2=None, op0=ALU.mult, saturate=False
-                            )
-                        k += 1
-                        if k == 14:
-                            nc.sync.dma_start(
-                                out=out_1[bt * P : (bt + 1) * P, 8 * h : 8 * h + 4, :].rearrange("b n m -> b (n m)"),
-                                in_=f8[:, 0:2048].bitcast(U8),
-                            )
-                    if k < 16:
-                        nc.sync.dma_start(
-                            out=out_1[bt * P : (bt + 1) * P, 8 * h : 8 * h + 8, :].rearrange("b n m -> b (n m)"),
-                            in_=f8[:].bitcast(U8),
-                        )
-                    else:
-                        nc.sync.dma_start(
-                            out=out_1[bt * P : (bt + 1) * P, 8 * h + 4 : 8 * h + 8, :].rearrange("b n m -> b (n m)"),
-                            in_=f8[:, 2048:4096].bitcast(U8),
-                        )
+                    f8[(bt, h)] = f8p.tile([P, half], FP8, name="f8_%d_%d" % (bt, h))
+
+            def cast(eng, bt, h, c0, c1):
+                dst = f8[(bt, h)][:, c0:c1]
+                src = obig[bt][:, h * half + c0 : h * half + c1]
+                if eng == "S":
+                    nc.scalar.activation(
+                        out=dst, in_=src, func=ACT.Identity, scale=fac[:, 0:1], bias=zeros[:, 0:1], saturate=False
+                    )
+                else:
+                    nc.vector.tensor_scalar(
+                        out=dst, in0=src, scalar1=fac[:, 0:1], scalar2=None, op0=ALU.mult, saturate=False
+                    )
+
+            def store(bt, h, c0, c1):
+                nc.sync.dma_start(
+                    out=out_1[bt * P : (bt + 1) * P, 8 * h + c0 // HM : 8 * h + c1 // HM, :].rearrange("b n m -> b (n m)"),
+                    in_=f8[(bt, h)][:, c0:c1].bitcast(U8),
+                )
+
+            cast("V", 0, 0, 0, 2048)
+            cast("S", 0, 0, 2048, 3072)
+            cast("V", 0, 0, 3072, 4096)
+            store(0, 0, 0, half)
+            cast("S", 0, 1, 0, 1024)
+            cast("V", 0, 1, 1024, 3072)
+            cast("S", 0, 1, 3072, 4096)
+            store(0, 1, 0, half)
+            cast("V", 1, 0, 0, 2048)
+            cast("S", 1, 0, 2048, 3072)
+            cast("V", 1, 0, 3072, 4096)
+            store(1, 0, 0, half)
+            cast("S", 1, 1, 0, 1024)
+            cast("V", 1, 1, 1024, 2048)
+            store(1, 1, 0, 2048)
+            cast("V", 1, 1, 2048, 3584)
+            cast("S", 1, 1, 3584, 4096)
+            store(1, 1, 2048, 4096)

@@ -31,6 +31,8 @@ LATE = [5, 7]
 J_BANK = [1, 2, 4, 5, 7, 8, 10, 11]
 J_QIN = 13
 WIDE = False
+VADD = 2
+G_OLD = False
 
 
 def tile_tensormoe_pa_kernel(tc, x, W_im, W_in, leak_m, leak_n, out_0, out_1):
@@ -153,7 +155,11 @@ def tile_tensormoe_pa_kernel(tc, x, W_im, W_in, leak_m, leak_n, out_0, out_1):
             def interleave(eng, pair, g, nl, m0, m1):
                 src = rawim[pair][:, nl, :, m0:m1].rearrange("p j (c i) -> p c j i", i=4)
                 dst = g[:, nl * 4 * HM + 4 * m0 : nl * 4 * HM + 4 * m1].rearrange("p (c i j) -> p c j i", i=4, j=4)
-                if eng == "G":
+                if eng == "G" and G_OLD:
+                    src = rawim[pair][:, nl, :, m0:m1].rearrange("p j m -> p m j")
+                    dst = g[:, nl * 4 * HM + 4 * m0 : nl * 4 * HM + 4 * m1].rearrange("p (m j) -> p m j", j=4)
+                    nc.gpsimd.tensor_scalar(out=dst, in0=src, scalar1=1.0, scalar2=0.0, op0=ALU.mult, op1=ALU.add)
+                elif eng == "G":
                     nc.gpsimd.tensor_scalar(out=dst, in0=src, scalar1=1.0, scalar2=0.0, op0=ALU.mult, op1=ALU.add)
                 elif eng == "S":
                     nc.scalar.copy(out=dst, in_=src)
@@ -275,12 +281,21 @@ def tile_tensormoe_pa_kernel(tc, x, W_im, W_in, leak_m, leak_n, out_0, out_1):
                 nc.vector.scalar_tensor_tensor(
                     out=uu[:, hs], in0=nq, scalar=en[:, n : n + 1], in1=sb[:], op0=ALU.mult, op1=ALU.add
                 )
+                if j >= HN * BT - VADD:
+                    return
                 if j // 4 == NU - 1 or not WIDE:
                     osl = oslice(n, bt)
                     nc.gpsimd.tensor_tensor(out=osl, in0=uu[:, hs], in1=osl, op=ALU.add)
                 elif j % 2 == 1:
                     o = otile[(n // 2, bt)]
                     nc.gpsimd.tensor_tensor(out=o, in0=uu, in1=o, op=ALU.add)
+
+            def v_add(j):
+                n, bt = tile_of(j)
+                uu = rings["uu"][:, (j // 2) % 2, :]
+                hs = slice((n % 2) * HM, (n % 2 + 1) * HM)
+                osl = oslice(n, bt)
+                nc.vector.tensor_tensor(out=osl, in0=uu[:, hs], in1=osl, op=ALU.add)
 
             def finish(j):
                 n, bt = tile_of(j)
@@ -330,7 +345,12 @@ def tile_tensormoe_pa_kernel(tc, x, W_im, W_in, leak_m, leak_n, out_0, out_1):
                 if k >= 1 and TB[k - 1] is not None:
                     q_in(TB[k - 1])
                 q_im(k)
-                p_mm(k)
+                p_one(2 * k, 0)
+                p_one(2 * k, 1)
+                if k >= 1:
+                    b_pass(2 * k - 1)
+                p_one(2 * k + 1, 0)
+                p_one(2 * k + 1, 1)
                 if TB[k] is not None:
                     for r in range(4):
                         if T2_ENGINES[r] == "S" or k not in V_STEPS:
@@ -346,11 +366,11 @@ def tile_tensormoe_pa_kernel(tc, x, W_im, W_in, leak_m, leak_n, out_0, out_1):
                         if T2_ENGINES[r] != "S" and k in V_STEPS:
                             t2_copy(TB[k], r)
                 b_pass(2 * k)
-                b_pass(2 * k + 1)
 
             k = NL1
             q_in(TB[k - 1])
             q_im(k)
+            b_pass(2 * k - 1)
             rings["uu"] = rawim_pool.tile([P, 2, 2 * HM], F32, name="uuring", tag="rawim")
 
             NJ = HN * BT
@@ -388,7 +408,10 @@ def tile_tensormoe_pa_kernel(tc, x, W_im, W_in, leak_m, leak_n, out_0, out_1):
                     served += 1
                 for f in fill.get(j, []):
                     f()
-            for item in pending[served:]:
+            late_adds = list(range(NJ - VADD, NJ))
+            for q, item in enumerate(pending[served:]):
+                if q < len(late_adds):
+                    v_add(late_adds[q])
                 finish(item[1])
 
         nc.vector.tensor_reduce(out=part[:], in_=stats[:], axis=AX.X, op=ALU.max)

@@ -20,11 +20,12 @@ MT = HM // P
 NU = HN // 2
 FLOPS = 2 * B * K * (2 * HN * HM)
 
-S_M = 384
+S_M = 480
+S_M0, S_O0 = 512, 64
 T2_ENGINES = "SSSV"
 REDUCE_DELAY = 3
 AHEAD = 2
-V_STEPS = (1, 3, 5)
+V_STEPS = (1, 2, 3, 4, 5, 6)
 NL1 = 7
 TB = [None, 0, 1, 2, 3, 4, 6]
 LATE = [5, 7]
@@ -356,9 +357,13 @@ def tile_tensormoe_pa_kernel(tc, x, W_im, W_in, leak_m, leak_n, out_0, out_1):
                         if T2_ENGINES[r] == "S" or k not in V_STEPS:
                             t2_copy(TB[k], r, "S")
                 g = new_stgim(k + 1)
-                interleave("G", k + 1, g, 1, 0, HM)
-                interleave("G", k + 1, g, 0, S_M, HM)
-                interleave("S", k + 1, g, 0, 0, S_M)
+                s_even, s_odd = (S_M0, S_O0) if k == 0 else (S_M, 0)
+                interleave("G", k + 1, g, 1, s_odd, HM)
+                if s_even < HM:
+                    interleave("G", k + 1, g, 0, s_even, HM)
+                interleave("S", k + 1, g, 0, 0, s_even)
+                if s_odd > 0:
+                    interleave("S", k + 1, g, 1, 0, s_odd)
                 done_t3.add(k + 1)
                 pump()
                 if TB[k] is not None:

@@ -30,8 +30,10 @@ NL1 = 7
 TB = [None, 0, 1, 2, 3, 4, 6]
 LATE = [5, 7]
 J_BANK = [1, 2, 4, 5, 7, 8, 10, 11]
-J_QIN = 13
-WIDE = False
+J_QIN = 12
+WIDE = True
+NRING = 3
+J_LEAD3 = 12
 VADD = 2
 G_OLD = False
 
@@ -269,7 +271,7 @@ def tile_tensormoe_pa_kernel(tc, x, W_im, W_in, leak_m, leak_n, out_0, out_1):
                         rhs=cin[:, mt, ns].bitcast(FP8X4), rhs_scale=sc_in[:, mt, ns],
                         start=False, stop=True,
                     )
-                nqt = prep.tile([P, HM], F32, name="nq%d" % j, tag="pa" if j % 2 == 0 else "pc", align_bytes=64)
+                nqt = prep.tile([P, HM], F32, name="nq%d" % j, tag=("pa", "pc", "pe")[j % 3], align_bytes=64)
                 nq = nqt[:]
                 nc.scalar.activation(out=nq, in_=qb[:], func=ACT.Relu, scale=-1.0)
                 banks[j] = (nq, sb)
@@ -277,7 +279,7 @@ def tile_tensormoe_pa_kernel(tc, x, W_im, W_in, leak_m, leak_n, out_0, out_1):
             def epi(j):
                 n, bt = tile_of(j)
                 nq, sb = banks[j]
-                uu = rings["uu"][:, (j // 2) % 2, :]
+                uu = rings["uu"][(j // 4) % NRING][:, (j // 2) % 2, :]
                 hs = slice((n % 2) * HM, (n % 2 + 1) * HM)
                 nc.vector.scalar_tensor_tensor(
                     out=uu[:, hs], in0=nq, scalar=en[:, n : n + 1], in1=sb[:], op0=ALU.mult, op1=ALU.add
@@ -293,7 +295,7 @@ def tile_tensormoe_pa_kernel(tc, x, W_im, W_in, leak_m, leak_n, out_0, out_1):
 
             def v_add(j):
                 n, bt = tile_of(j)
-                uu = rings["uu"][:, (j // 2) % 2, :]
+                uu = rings["uu"][(j // 4) % NRING][:, (j // 2) % 2, :]
                 hs = slice((n % 2) * HM, (n % 2 + 1) * HM)
                 osl = oslice(n, bt)
                 nc.vector.tensor_tensor(out=osl, in0=uu[:, hs], in1=osl, op=ALU.add)
@@ -376,7 +378,9 @@ def tile_tensormoe_pa_kernel(tc, x, W_im, W_in, leak_m, leak_n, out_0, out_1):
             q_in(TB[k - 1])
             q_im(k)
             b_pass(2 * k - 1)
-            rings["uu"] = rawim_pool.tile([P, 2, 2 * HM], F32, name="uuring", tag="rawim")
+            rings["uu"] = []
+            for q in range(NRING):
+                rings["uu"].append(rawim_pool.tile([P, 2, 2 * HM], F32, name="uuring%d" % q, tag="rawim"))
 
             NJ = HN * BT
             fill = {}
@@ -402,9 +406,11 @@ def tile_tensormoe_pa_kernel(tc, x, W_im, W_in, leak_m, leak_n, out_0, out_1):
                 mm(j)
             pending = []
             served = 0
+            made = AHEAD
             for j in range(NJ):
-                if j + AHEAD < NJ:
-                    mm(j + AHEAD)
+                while made < NJ and made <= j + (AHEAD if j < J_LEAD3 else AHEAD + 1):
+                    mm(made)
+                    made += 1
                 epi(j)
                 if j % 2 == 1 or j // 4 == NU - 1:
                     pending.append((j + REDUCE_DELAY, j))

from contextlib import ExitStack

import concourse.mybir as mybir
from concourse.masks import make_identity

F32 = mybir.dt.float32
BF16 = mybir.dt.bfloat16
U32 = mybir.dt.uint32
U8 = mybir.dt.uint8
FP8X4 = mybir.dt.float8_e4m3fn_x4
FP8 = mybir.dt.float8_e4m3fn
ALU = mybir.AluOpType
ACT = mybir.ActivationFunctionType
AX = mybir.AxisListType

B, K, HM, HN = 256, 512, 512, 16
P = 128
BT = B // P
MT = HM // P
NU = HN // 2
FLOPS = 2 * B * K * (2 * HN * HM)

S_M = 480
S_M0, S_O0 = 512, 64
T2_ENGINES = "SSSV"
REDUCE_DELAY = 3
AHEAD = 2
V_STEPS = (1, 2, 3, 4, 5, 6)
NL1 = 7
TB = [None, 0, 1, 2, 3, 4, 6]
LATE = [5, 7]
J_BANK = [1, 2, 4, 5, 7, 8, 10, 11]
J_QIN = 12
WIDE = True
NRING = 3
J_LEAD3 = 12
VADD = 2
G_OLD = False


def tile_tensormoe_pa_kernel(tc, x, W_im, W_in, leak_m, leak_n, out_0, out_1):
    nc = tc.nc
    with ExitStack() as ctx:
        const = ctx.enter_context(tc.tile_pool(name="const", bufs=1))
        outp = ctx.enter_context(tc.tile_pool(name="outp", bufs=1))
        psum = ctx.enter_context(tc.psum_pool(name="psum", bufs=4))

        zeros = const.tile([P, 1], F32, name="zeros")
        nc.vector.memset(zeros[:], 0.0)
        warm = const.tile([P, 1], F32, name="warm")
        nc.scalar.activation(out=warm[:], in_=zeros[:], func=ACT.Relu)
        ident = const.tile([P, P], F32, name="ident")
        make_identity(nc, ident[:])

        cin = const.tile([P, MT, HN * P], U32, name="cin", align_bytes=64)
        sc_in = const.tile([P, MT, HN * P], U8, name="sc_in", align_bytes=64)
        cim = const.tile([P, HN * HM], U32, name="cim", align_bytes=64)
        sc_im = const.tile([P, HN * HM], U8, name="sc_im", align_bytes=64)
        xq = const.tile([P, B], U32, name="xq", align_bytes=64)
        xs = const.tile([P, B], U8, name="xs", align_bytes=64)
        dm = const.tile([P, HM], F32, name="dm")
        en = const.tile([P, HN], F32, name="en")
        stats = const.tile([P, HN + 2], F32, name="stats")
        part = const.tile([P, 1], F32, name="part")
        amax = const.tile([P, 1], F32, name="amax")
        rec = const.tile([P, 1], F32, name="rec")
        fac = const.tile([P, 1], F32, name="fac")

        obig = []
        for bt in range(BT):
            obig.append(outp.tile([P, HN * HM], F32, name="obig%d" % bt))
        otile = {}
        for nu in range(NU):
            for bt in range(BT):
                otile[(nu, bt)] = obig[bt][:, nu * 2 * HM : (nu + 1) * 2 * HM]

        def oslice(n, bt):
            return otile[(n // 2, bt)][:, (n % 2) * HM : (n % 2 + 1) * HM]

        def xop(bt):
            bs = slice(bt * P, (bt + 1) * P)
            return xq[:, bs].bitcast(FP8X4), xs[:, bs]

        sched = ctx.enter_context(tc.manual_schedule())

        with ExitStack() as pctx:
            prep = pctx.enter_context(tc.tile_pool(name="prep", bufs=1))
            rawim_pool = pctx.enter_context(tc.tile_pool(name="rawim", bufs=3))
            stgim_pool = pctx.enter_context(tc.tile_pool(name="stgim", bufs=1))
            rawin_pool = pctx.enter_context(tc.tile_pool(name="rawin", bufs=2))
            stgin_pool = pctx.enter_context(tc.tile_pool(name="stgin", bufs=2))

            x_sb = prep.tile([P, BT, K], BF16, name="x_sb", tag="pa", align_bytes=64)
            nc.sync.dma_start(out=x_sb[:], in_=x.rearrange("(t p) k -> p t k", p=P))
            lrow = prep.tile([P, HM + HN], BF16, name="lrow")
            nc.vector.memset(lrow[:], 0.0)
            ones = prep.tile([P, P], BF16, name="ones")
            nc.vector.memset(ones[:], 1.0)
            nc.sync.dma_start(out=lrow[0:1, 0:HM], in_=leak_m.rearrange("(o m) -> o m", o=1))
            nc.sync.dma_start(out=lrow[0:1, HM : HM + HN], in_=leak_n.rearrange("(o n) -> o n", o=1))

            rawim = {}
            rawin = {}
            done_t3 = set()
            done_blk = set()
            order = [
                ("im", 0), ("im", 1), ("in", 0), ("im", 2), ("im", 3), ("in", 1), ("im", 4), ("in", 2),
                ("im", 5), ("im", 6), ("in", 3), ("im", 7),
            ]
            head = [0]

            def pump():
                while head[0] < len(order):
                    kind, j = order[head[0]]
                    if kind == "im":
                        if j >= 3 and (j - 3) not in done_t3:
                            return
                        t = rawim_pool.tile([P, 2, 4, HM], BF16, name="rawim%d" % j, tag="rawim")
                        nc.sync.dma_start(
                            out=t[:], in_=W_im[2 * j : 2 * j + 2].rearrange("n (p j) m -> p n j m", j=4)
                        )
                        rawim[j] = t
                    else:
                        if j >= 2 and (2 * (j - 2) + 1) not in done_blk:
                            return
                        t = rawin_pool.tile([P, K * HN], BF16, name="rawin%d" % j, tag="rawin")
                        half = K * HN // 2
                        srcv = W_in[j * P : (j + 1) * P].rearrange("m i n -> m (i n)")
                        for h in range(2):
                            nc.sync.dma_start(
                                out=t[:, h * half : (h + 1) * half], in_=srcv[:, h * half : (h + 1) * half]
                            )
                        rawin[j] = t
                    head[0] += 1

            pump()

            xt = psum.tile([P, BT, 2, P], F32, name="xt", tag="tp")
            for bt in range(BT):
                xw = x_sb[:, bt, :].bitcast(F32)
                for u in range(2):
                    nc.tensor.transpose(xt[:, bt, u, :], xw[:, u::2], ident[:])
            lmp = psum.tile([P, HM], F32, name="lmp", tag="pb")
            nc.tensor.matmul(out=lmp[:], lhsT=ones[:], rhs=lrow[:, 0:HM], start=True, stop=True)
            lnp = psum.tile([P, HN], F32, name="lnp", tag="pb")
            nc.tensor.matmul(out=lnp[:], lhsT=ones[:], rhs=lrow[:, HM : HM + HN], start=True, stop=True)
            gx = prep.tile([P, B * 4], BF16, name="gx", tag="pc", align_bytes=64)
            nc.vector.tensor_copy(
                out=gx[:].bitcast(F32).rearrange("p (t b u) -> p t b u", t=BT, u=2),
                in_=xt[:].rearrange("p t u b -> p t b u"),
            )
            nc.vector.tensor_scalar(out=dm[:], in0=lmp[:], scalar1=-1.0, scalar2=None, op0=ALU.add)
            nc.vector.quantize_mx(out=xq[:].bitcast(FP8X4), scales=xs[:], in_=gx[:])
            nc.vector.tensor_scalar(out=en[:], in0=lnp[:], scalar1=-1.0, scalar2=1.0, op0=ALU.mult, op1=ALU.add)

            stgim = {}

            def interleave(eng, pair, g, nl, m0, m1):
                src = rawim[pair][:, nl, :, m0:m1].rearrange("p j (c i) -> p c j i", i=4)
                dst = g[:, nl * 4 * HM + 4 * m0 : nl * 4 * HM + 4 * m1].rearrange("p (c i j) -> p c j i", i=4, j=4)
                if eng == "G" and G_OLD:
                    src = rawim[pair][:, nl, :, m0:m1].rearrange("p j m -> p m j")
                    dst = g[:, nl * 4 * HM + 4 * m0 : nl * 4 * HM + 4 * m1].rearrange("p (m j) -> p m j", j=4)
                    nc.gpsimd.tensor_scalar(out=dst, in0=src, scalar1=1.0, scalar2=0.0, op0=ALU.mult, op1=ALU.add)
                elif eng == "G":
                    nc.gpsimd.tensor_scalar(out=dst, in0=src, scalar1=1.0, scalar2=0.0, op0=ALU.mult, op1=ALU.add)
                elif eng == "S":
                    nc.scalar.copy(out=dst, in_=src)
                else:
                    nc.vector.tensor_copy(out=dst, in_=src)

            def new_stgim(pair):
                stgim[pair] = stgim_pool.tile([P, 8 * HM], BF16, name="stgim%d" % pair, tag="stgim", align_bytes=64)
                return stgim[pair]

            def q_im(pair):
                cs = slice(pair * 2 * HM, (pair + 1) * 2 * HM)
                nc.vector.quantize_mx(out=cim[:, cs].bitcast(FP8X4), scales=sc_im[:, cs], in_=stgim[pair][:])

            pbank = {}

            def p_mm(pair):
                for n in (2 * pair, 2 * pair + 1):
                    cs = slice(n * HM, (n + 1) * HM)
                    for bt in range(BT):
                        lhsT, lsc = xop(bt)
                        pb = psum.tile([P, HM], F32, name="pb%d_%d" % (n, bt), tag="pb")
                        nc.tensor.matmul_mx(
                            out=pb[:], lhsT=lhsT, lhsT_scale=lsc,
                            rhs=cim[:, cs].bitcast(FP8X4), rhs_scale=sc_im[:, cs],
                            start=True, stop=True,
                        )
                        pbank[(n, bt)] = pb

            def b_pass(n):
                for bt in range(BT):
                    nc.vector.scalar_tensor_tensor(
                        out=oslice(n, bt), in0=pbank[(n, bt)][:], scalar=0.0, in1=dm[:],
                        op0=ALU.min, op1=ALU.mult,
                    )

            tbank = {}
            stgin = {}

            def t2_transposes(blk):
                mt, h = blk // 2, blk % 2
                words = rawin[mt][:].bitcast(F32)
                for r in range(4):
                    nu = 4 * h + r
                    tp = psum.tile([P, 4, P], F32, name="tp%d_%d" % (mt, nu), tag="tp")
                    for t in range(4):
                        nc.tensor.transpose(tp[:, t, :], words[:, 8 * t + nu :: 32], ident[:])
                    tbank[(blk, r)] = tp
                done_blk.add(blk)
                pump()

            def t2_tr_one(blk, r):
                mt, h = blk // 2, blk % 2
                words = rawin[mt][:].bitcast(F32)
                nu = 4 * h + r
                tp = psum.tile([P, 4, P], F32, name="tp%d_%d" % (mt, nu), tag="tp")
                for t in range(4):
                    nc.tensor.transpose(tp[:, t, :], words[:, 8 * t + nu :: 32], ident[:])
                tbank[(blk, r)] = tp

            def t2_copy(blk, r, eng=None):
                if r == 0:
                    stgin[blk] = stgin_pool.tile([P, 4096], BF16, name="stgin%d" % blk, tag="stgin", align_bytes=64)
                tp = tbank[(blk, r)]
                src = tp[:].rearrange("p t m -> p (t m)").bitcast(BF16).rearrange("p (t m e) -> p e m t", t=4, e=2)
                dst = stgin[blk][:, r * 1024 : (r + 1) * 1024].rearrange("p (e m t) -> p e m t", e=2, t=4)
                if (eng or T2_ENGINES[r]) == "S":
                    nc.scalar.copy(out=dst, in_=src)
                else:
                    nc.vector.tensor_copy(out=dst, in_=src)

            def q_in(blk):
                mt, h = blk // 2, blk % 2
                cs = slice(h * 1024, (h + 1) * 1024)
                nc.vector.quantize_mx(out=cin[:, mt, cs].bitcast(FP8X4), scales=sc_in[:, mt, cs], in_=stgin[blk][:])

            banks = {}
            rings = {}

            def tile_of(j):
                return 2 * (j // 4) + j % 2, (j % 4) // 2

            def mm(j):
                n, bt = tile_of(j)
                lhsT, lsc = xop(bt)
                qb = psum.tile([P, HM], F32, name="qb%d_%d" % (n, bt), tag="tp")
                sb = psum.tile([P, HM], F32, name="sb%d_%d" % (n, bt), tag="pb")
                ns = slice(n * P, (n + 1) * P)
                for mt in range(MT):
                    ms = slice(mt * P, (mt + 1) * P)
                    nc.tensor.matmul_mx(
                        out=qb[:, ms], lhsT=lhsT, lhsT_scale=lsc,
                        rhs=cin[:, mt, ns].bitcast(FP8X4), rhs_scale=sc_in[:, mt, ns],
                        start=True, stop=True,
                    )
                for mt in range(MT):
                    ms = slice(mt * P, (mt + 1) * P)
                    cs = slice(n * HM + mt * P, n * HM + (mt + 1) * P)
                    nc.tensor.matmul_mx(
                        out=sb[:, ms], lhsT=lhsT, lhsT_scale=lsc,
                        rhs=cim[:, cs].bitcast(FP8X4), rhs_scale=sc_im[:, cs],
                        start=True, stop=False,
                    )
                    nc.tensor.matmul_mx(
                        out=sb[:, ms], lhsT=lhsT, lhsT_scale=lsc,
                        rhs=cin[:, mt, ns].bitcast(FP8X4), rhs_scale=sc_in[:, mt, ns],
                        start=False, stop=True,
                    )
                nqt = prep.tile([P, HM], F32, name="nq%d" % j, tag=("pa", "pc", "pe")[j % 3], align_bytes=64)
                nq = nqt[:]
                nc.scalar.activation(out=nq, in_=qb[:], func=ACT.Relu, scale=-1.0)
                banks[j] = (nq, sb)

            def epi(j):
                n, bt = tile_of(j)
                nq, sb = banks[j]
                uu = rings["uu"][(j // 4) % NRING][:, (j // 2) % 2, :]
                hs = slice((n % 2) * HM, (n % 2 + 1) * HM)
                nc.vector.scalar_tensor_tensor(
                    out=uu[:, hs], in0=nq, scalar=en[:, n : n + 1], in1=sb[:], op0=ALU.mult, op1=ALU.add
                )
                if j >= HN * BT - VADD:
                    return
                if j // 4 == NU - 1 or not WIDE:
                    osl = oslice(n, bt)
                    nc.gpsimd.tensor_tensor(out=osl, in0=uu[:, hs], in1=osl, op=ALU.add)
                elif j % 2 == 1:
                    o = otile[(n // 2, bt)]
                    nc.gpsimd.tensor_tensor(out=o, in0=uu, in1=o, op=ALU.add)

            def v_add(j):
                n, bt = tile_of(j)
                uu = rings["uu"][(j // 4) % NRING][:, (j // 2) % 2, :]
                hs = slice((n % 2) * HM, (n % 2 + 1) * HM)
                osl = oslice(n, bt)
                nc.vector.tensor_tensor(out=osl, in0=uu[:, hs], in1=osl, op=ALU.add)

            def finish(j):
                n, bt = tile_of(j)
                nu = n // 2
                o = otile[(nu, bt)]
                if nu < NU - 1:
                    c = nu * BT + bt
                    src = o
                else:
                    c = (NU - 1) * BT + j % 4
                    src = oslice(n, bt)
                nc.vector.tensor_reduce(
                    out=stats[:, c : c + 1], in_=src, axis=AX.X, op=ALU.max, apply_absolute_value=True
                )
                if j % 2 == 1:
                    nc.sync.dma_start(
                        out=out_0[bt * P : (bt + 1) * P, 2 * nu : 2 * nu + 2, :].rearrange("b n m -> b (n m)"),
                        in_=o,
                    )

            def p_one(n, bt):
                cs = slice(n * HM, (n + 1) * HM)
                lhsT, lsc = xop(bt)
                pb = psum.tile([P, HM], F32, name="pb%d_%d" % (n, bt), tag="pb")
                nc.tensor.matmul_mx(
                    out=pb[:], lhsT=lhsT, lhsT_scale=lsc,
                    rhs=cim[:, cs].bitcast(FP8X4), rhs_scale=sc_im[:, cs],
                    start=True, stop=True,
                )
                pbank[(n, bt)] = pb

            def b_one(n, bt):
                nc.vector.scalar_tensor_tensor(
                    out=oslice(n, bt), in0=pbank[(n, bt)][:], scalar=0.0, in1=dm[:],
                    op0=ALU.min, op1=ALU.mult,
                )

            g = new_stgim(0)
            interleave("V", 0, g, 0, 0, HM)
            interleave("S", 0, g, 1, 0, HM // 2)
            interleave("G", 0, g, 1, HM // 2, HM)
            done_t3.add(0)
            pump()
            for k in range(NL1):
                if TB[k] is not None:
                    t2_transposes(TB[k])
                if k >= 1 and TB[k - 1] is not None:
                    q_in(TB[k - 1])
                q_im(k)
                p_one(2 * k, 0)
                p_one(2 * k, 1)
                if k >= 1:
                    b_pass(2 * k - 1)
                p_one(2 * k + 1, 0)
                p_one(2 * k + 1, 1)
                if TB[k] is not None:
                    for r in range(4):
                        if T2_ENGINES[r] == "S" or k not in V_STEPS:
                            t2_copy(TB[k], r, "S")
                g = new_stgim(k + 1)
                s_even, s_odd = (S_M0, S_O0) if k == 0 else (S_M, 0)
                interleave("G", k + 1, g, 1, s_odd, HM)
                if s_even < HM:
                    interleave("G", k + 1, g, 0, s_even, HM)
                interleave("S", k + 1, g, 0, 0, s_even)
                if s_odd > 0:
                    interleave("S", k + 1, g, 1, 0, s_odd)
                done_t3.add(k + 1)
                pump()
                if TB[k] is not None:
                    for r in range(4):
                        if T2_ENGINES[r] != "S" and k in V_STEPS:
                            t2_copy(TB[k], r)
                b_pass(2 * k)

            k = NL1
            q_in(TB[k - 1])
            q_im(k)
            b_pass(2 * k - 1)
            rings["uu"] = []
            for q in range(NRING):
                rings["uu"].append(rawim_pool.tile([P, 2, 2 * HM], F32, name="uuring%d" % q, tag="rawim"))

            NJ = HN * BT
            fill = {}

            def at(j, f):
                fill.setdefault(j, []).append(f)

            def first_pass(n, bt):
                p_one(n, bt)
                b_one(n, bt)

            for q, (n, bt) in enumerate([(2 * k, 0), (2 * k + 1, 0), (2 * k, 1), (2 * k + 1, 1)]):
                at(q, lambda n=n, bt=bt: p_one(n, bt))
                at(q + 1, lambda n=n, bt=bt: b_one(n, bt))
            for q in range(8):
                blk, r = LATE[q // 4], q % 4
                at(J_BANK[q] - 1, lambda blk=blk, r=r: t2_tr_one(blk, r))
                at(J_BANK[q], lambda blk=blk, r=r: t2_copy(blk, r, "S"))
            at(J_QIN, lambda: q_in(LATE[0]))
            at(J_QIN, lambda: q_in(LATE[1]))

            for j in range(AHEAD):
                mm(j)
            pending = []
            served = 0
            made = AHEAD
            for j in range(NJ):
                while made < NJ and made <= j + (AHEAD if j < J_LEAD3 else AHEAD + 1):
                    mm(made)
                    made += 1
                epi(j)
                if j % 2 == 1 or j // 4 == NU - 1:
                    pending.append((j + REDUCE_DELAY, j))
                while served < len(pending) and pending[served][0] <= j:
                    finish(pending[served][1])
                    served += 1
                for f in fill.get(j, []):
                    f()
            late_adds = list(range(NJ - VADD, NJ))
            for q, item in enumerate(pending[served:]):
                if q < len(late_adds):
                    v_add(late_adds[q])
                finish(item[1])

        nc.vector.tensor_reduce(out=part[:], in_=stats[:], axis=AX.X, op=ALU.max)
        pt = psum.tile([P, P], F32, name="pt", tag="tp")
        nc.tensor.transpose(pt[:], part[:, 0:1].to_broadcast([P, P]), ident[:])
        nc.vector.tensor_reduce(out=amax[:], in_=pt[:], axis=AX.X, op=ALU.max)
        nc.vector.reciprocal(out=rec[:], in_=amax[:])
        nc.vector.tensor_scalar(out=fac[:], in0=rec[:], scalar1=448.0, scalar2=None, op0=ALU.mult)

        with tc.tile_pool(name="f8p", bufs=1) as f8p:
            half = HN * HM // 2
            f8 = {}
            for bt in range(BT):
                for h in range(2):
                    f8[(bt, h)] = f8p.tile([P, half], FP8, name="f8_%d_%d" % (bt, h))

            def cast(eng, bt, h, c0, c1):
                dst = f8[(bt, h)][:, c0:c1]
                src = obig[bt][:, h * half + c0 : h * half + c1]
                if eng == "S":
                    nc.scalar.activation(
                        out=dst, in_=src, func=ACT.Identity, scale=fac[:, 0:1], bias=zeros[:, 0:1], saturate=False
                    )
                else:
                    nc.vector.tensor_scalar(
                        out=dst, in0=src, scalar1=fac[:, 0:1], scalar2=None, op0=ALU.mult, saturate=False
                    )

            def store(bt, h, c0, c1):
                nc.sync.dma_start(
                    out=out_1[bt * P : (bt + 1) * P, 8 * h + c0 // HM : 8 * h + c1 // HM, :].rearrange("b n m -> b (n m)"),
                    in_=f8[(bt, h)][:, c0:c1].bitcast(U8),
                )

            cast("V", 0, 0, 0, 2048)
            cast("S", 0, 0, 2048, 3072)
            cast("V", 0, 0, 3072, 4096)
            store(0, 0, 0, half)
            cast("S", 0, 1, 0, 1024)
            cast("V", 0, 1, 1024, 3072)
            cast("S", 0, 1, 3072, 4096)
            store(0, 1, 0, half)
            cast("V", 1, 0, 0, 2048)
            cast("S", 1, 0, 2048, 3072)
            cast("V", 1, 0, 3072, 4096)
            store(1, 0, 0, half)
            cast("S", 1, 1, 0, 1024)
            cast("V", 1, 1, 1024, 2048)
            store(1, 1, 0, 2048)
            cast("V", 1, 1, 2048, 3584)
            cast("S", 1, 1, 3584, 4096)
            store(1, 1, 2048, 4096)
